import numpy as np
import ml_dtypes


def mxq(x, axis, fmt="e4m3"):
    dtype, down = {"e4m3": (ml_dtypes.float8_e4m3fn, 7), "e5m2": (ml_dtypes.float8_e5m2, 14)}[fmt]
    v = np.moveaxis(np.asarray(x, np.float32).astype(ml_dtypes.bfloat16).astype(np.float64), axis, -1)
    blocks = v.reshape(v.shape[:-1] + (-1, 32))
    amax = np.abs(blocks).max(-1, keepdims=True)
    byte = np.maximum(np.where(amax > 0, np.frexp(amax)[1] - 1 + 127, 0) - down, 1)
    scale = np.exp2(byte - 127.0)
    codes = (blocks / scale).astype(np.float32).astype(dtype).astype(np.float64)
    return np.moveaxis((codes * scale).reshape(v.shape), -1, axis)


WIDE = False


def mx_kscale(k):
    if not WIDE:
        return np.ones(k)
    levels = np.array([10, -10, 5, -5, 0])
    if k % 512:
        return np.exp2(np.random.permutation(np.resize(levels, k // 32))).repeat(32)
    a = np.empty((k // 512, 16))
    for p in range(k // 512):
        a[p, :8] = np.random.permutation(np.resize(levels, 8))
        for g in range(8):
            far = levels[np.abs(levels - a[p, g]) >= 10]
            a[p, g + 8] = far[np.random.randint(len(far))]
    return np.exp2(a.ravel()).repeat(32)


BF16 = ml_dtypes.bfloat16


def bf(x):
    return np.asarray(x, np.float32).astype(BF16)


def f64(x):
    return np.asarray(x).astype(np.float64)


B, S, D = 32, 256, 512
NB = 2
W = 2 * NB + 1
LN_EPS = 1e-5


def setup_inputs():
    s = mx_kscale(D)
    u = s / s.max()
    pos = np.arange(S)[:, None] + np.arange(W)[None, :] - NB
    e = np.exp(np.random.standard_normal((B, S, W))) * ((pos >= 0) & (pos < S))
    return {"x": bf(np.random.standard_normal((B, S, D)) * u),
            "Wv": bf(np.random.standard_normal((D, D)) / np.sqrt(D) / u[None, :]),
            "bv": bf(0.2 + 0.2 * np.random.standard_normal(D)),
            "attn_band": bf(e / e.sum(-1, keepdims=True)),
            "gamma": bf(1.0 + 0.1 * np.random.standard_normal(D)),
            "beta": bf(0.2 * np.random.standard_normal(D))}


def reference(x, Wv, bv, attn_band, gamma, beta):
    xf, a = f64(x), f64(attn_band)
    v = (mxq(xf, 2, "e4m3") @ mxq(f64(Wv), 1, "e4m3").T) + f64(bv)
    mix = np.zeros_like(xf)
    for j in range(W):
        o = j - NB
        lo, hi = max(0, -o), S - max(0, o)
        mix[:, lo:hi] += a[:, lo:hi, j:j + 1] * v[:, lo + o:hi + o]
    out = mix + xf
    mu = out.mean(-1, keepdims=True)
    var = out.var(-1, keepdims=True)
    return (out - mu) / np.sqrt(var + LN_EPS) * f64(gamma) + f64(beta)

@@ -1,0 +1,375 @@
+from contextlib import ExitStack
+
+import concourse.mybir as mybir
+from concourse.masks import make_identity
+
+F32 = mybir.dt.float32
+BF16 = mybir.dt.bfloat16
+U32 = mybir.dt.uint32
+U8 = mybir.dt.uint8
+I32 = mybir.dt.int32
+FP8X4 = mybir.dt.float8_e4m3fn_x4
+ALU = mybir.AluOpType
+ACT = mybir.ActivationFunctionType
+AX = mybir.AxisListType
+
+P = 128
+D = 512
+ROWS = 8192
+RUN = ROWS // P
+TAPS = 5
+NB = 2
+GRP = 4
+EPS = 1e-5
+CHUNKS = [2, 6, 8, 8, 8, 8, 8, 8, 8]
+TAIL = 8
+
+FLOPS = 2 * ROWS * D * D + 2 * ROWS * TAPS * D
+
+
+def tile_crosssliceattention_pb_t_kernel(tc, x, Wv, bv, attn_band, gamma, beta, out):
+    nc = tc.nc
+    xf = x.flatten_outer_dims()
+    x_rows = xf.rearrange("(p t) d -> p t d", t=RUN)
+    o_rows = out.flatten_outer_dims().rearrange("(p t) d -> p t d", t=RUN)
+
+    with ExitStack() as ctx:
+        const = ctx.enter_context(tc.tile_pool(name="const", bufs=1))
+        grp_pool = ctx.enter_context(tc.tile_pool(name="grp", bufs=2))
+        acc_pool = ctx.enter_context(tc.tile_pool(name="accp", bufs=18))
+        junk_pool = ctx.enter_context(tc.tile_pool(name="junkp", bufs=2))
+        stat_pool = ctx.enter_context(tc.tile_pool(name="statp", bufs=5))
+        big_pool = ctx.enter_context(tc.tile_pool(name="bigp", bufs=2))
+        out_pool = ctx.enter_context(tc.tile_pool(name="outp", bufs=3))
+        psx = ctx.enter_context(tc.psum_pool(name="psx", bufs=1))
+        psv = ctx.enter_context(tc.psum_pool(name="psv", bufs=3))
+        psf = ctx.enter_context(tc.psum_pool(name="psf", bufs=2))
+        psb = ctx.enter_context(tc.psum_pool(name="psb", bufs=2))
+        ctx.enter_context(tc.manual_schedule())
+
+        w_raw = const.tile([P, GRP, D], BF16, name="w_raw")
+        nc.sync.dma_start(out=w_raw[:], in_=Wv.rearrange("(c p) k -> p c k", p=P))
+        halo = const.tile([P, 2 * NB, D], BF16, name="halo")
+        nc.vector.memset(halo[:].bitcast(I32), 0)
+        lo_view = xf[RUN - NB : RUN - NB + RUN * (P - 1), :].rearrange("(p t) d -> p t d", t=RUN)
+        hi_view = xf[RUN:ROWS, :].rearrange("(p t) d -> p t d", t=RUN)
+        nc.sync.dma_start(out=halo[1:113, 0:NB, :], in_=lo_view[0:112, 0:NB, :])
+        nc.sync.dma_start(out=halo[113:128, 0:NB, :], in_=lo_view[112:127, 0:NB, :])
+        x_home = {}
+        first = 0
+        for n_tiles in CHUNKS:
+            t = const.tile([P, n_tiles, D], BF16, name="xc%d" % first)
+            nc.sync.dma_start(out=t[:], in_=x_rows[:, first : first + n_tiles, :])
+            for i in range(n_tiles):
+                x_home[first + i] = t[:, i, :]
+            first += n_tiles
+        nc.sync.dma_start(out=halo[0:112, NB : 2 * NB, :], in_=hi_view[0:112, 0:NB, :])
+        nc.sync.dma_start(out=halo[112:127, NB : 2 * NB, :], in_=hi_view[112:127, 0:NB, :])
+        gamma_b = const.tile([P, D], BF16, name="gamma_b")
+        nc.sync.dma_start(out=gamma_b[:], in_=gamma.partition_broadcast(P))
+        beta_b = const.tile([P, D], BF16, name="beta_b")
+        nc.sync.dma_start(out=beta_b[:], in_=beta.partition_broadcast(P))
+
+        a_bf = const.tile([P, RUN * TAPS], BF16, name="a_bf")
+        nc.scalar.dma_start(
+            out=a_bf[:], in_=attn_band.flatten_outer_dims().rearrange("(p t) j -> p (t j)", t=RUN)
+        )
+        bvb = const.tile([P, D], BF16, name="bvb")
+        nc.scalar.dma_start(out=bvb[:], in_=bv.partition_broadcast(P))
+        gbrow = const.tile([P, P], BF16, name="gbrow")
+        nc.vector.memset(gbrow[:], 0.0)
+        nc.scalar.dma_start(out=gbrow[0:4, :], in_=gamma.rearrange("(c p) -> c p", p=P))
+        nc.scalar.dma_start(out=gbrow[4:8, :], in_=beta.rearrange("(c p) -> c p", p=P))
+
+        ident_f = const.tile([P, P], F32, name="ident_f")
+        make_identity(nc, ident_f[:])
+        ident_b = const.tile([P, P], BF16, name="ident_b")
+        make_identity(nc, ident_b[:])
+
+        mhalf = const.tile([P, GRP], F32, name="mhalf")
+        nc.vector.memset(mhalf[:], -0.5)
+
+        def x_tile(i):
+            if i < 0:
+                return halo[:, i + NB, :]
+            if i >= RUN:
+                return halo[:, i - RUN + NB, :]
+            return x_home[i]
+
+        a_f = const.tile([P, RUN, TAPS], F32, name="a_f")
+        nc.vector.tensor_copy(out=a_f[:].rearrange("p t j -> p (t j)"), in_=a_bf[:])
+        csum = const.tile([P, RUN], F32, name="csum")
+        nc.vector.reduce_sum(out=csum[:], in_=a_f[:], axis=AX.X)
+
+        gb = const.tile([P, 8], F32, name="gb")
+
+        grouped = {}
+        xt_ps = {}
+
+        def turn(key, srcs, h, pool, tag):
+            xt = pool.tile([P, 2, 2, P], F32, name="xt", tag=tag)
+            for a in range(2):
+                w32 = srcs[2 * h + a].bitcast(F32)
+                for u in range(2):
+                    nc.tensor.transpose(
+                        out=xt[:, a, u, :], in_=w32[:, u : D // 2 : 2], identity=ident_f[:]
+                    )
+            xt_ps[(key, h)] = xt
+
+        def regroup(key, h, engine_copy):
+            if h == 0:
+                grouped[key] = grp_pool.tile([P, GRP * D], BF16, name="grouped", align_bytes=64)
+            g32 = grouped[key][:].bitcast(F32).rearrange("p (a t u) -> p a t u", a=GRP, u=2)
+            engine_copy(
+                out=g32[:, 2 * h : 2 * h + 2, :, :], in_=xt_ps[(key, h)][:].rearrange("p a u t -> p a t u")
+            )
+
+        def quantise(key, codes, scales):
+            nc.vector.quantize_mx(out=codes.bitcast(FP8X4), scales=scales, in_=grouped[key][:])
+
+        w_codes = const.tile([P, D], U32, name="w_codes", align_bytes=64)
+        w_scales = const.tile([P, D], U8, name="w_scales", align_bytes=64)
+        w_srcs = [w_raw[:, c, :] for c in range(GRP)]
+        for h in range(2):
+            turn("w", w_srcs, h, psf, "f_ps")
+        for h in range(2):
+            regroup("w", h, nc.scalar.copy)
+
+        NT = RUN + 2 * NB
+        NG_IN = NT // GRP
+        NG = RUN // GRP
+
+        def x_srcs(g):
+            return [x_tile(GRP * g - NB + a) for a in range(GRP)]
+
+        codes = {}
+        scales = {}
+
+        def quantise_x(g):
+            codes[g] = grp_pool.tile([P, D], U32, name="codes", align_bytes=64)
+            scales[g] = grp_pool.tile([P, D], U8, name="scales", align_bytes=64)
+            quantise(g, codes[g][:], scales[g][:])
+
+        for h in range(2):
+            turn(0, x_srcs(0), h, psb, "b_ps")
+        for h in range(2):
+            regroup(0, h, nc.vector.tensor_copy)
+        quantise("w", w_codes[:], w_scales[:])
+        quantise_x(0)
+
+        v_ps = {}
+        acc = {}
+        sums = {}
+        ssq = {}
+        mu = {}
+        rstd = {}
+        nrm = {}
+        y_t = {}
+        o_sb = {}
+        f_ps = {}
+        b_ps = {}
+
+        def project(k):
+            g, a = divmod(k, GRP)
+            v_ps[k] = psv.tile([P, D], F32, name="v_ps")
+            nc.tensor.matmul_mx(
+                out=v_ps[k][:],
+                lhsT=codes[g][:, a * P : (a + 1) * P].bitcast(FP8X4),
+                lhsT_scale=scales[g][:, a * P : (a + 1) * P],
+                rhs=w_codes[:].bitcast(FP8X4),
+                rhs_scale=w_scales[:],
+                start=True,
+                stop=True,
+            )
+
+        def taps(k):
+            for j in range(TAPS - 1, -1, -1):
+                m = k - j
+                if 0 <= m < RUN:
+                    g, a = divmod(m, GRP)
+                    nc.vector.scalar_tensor_tensor(
+                        out=acc[m][:],
+                        in0=v_ps[k][:],
+                        scalar=a_f[:, m, j : j + 1],
+                        in1=acc[m][:],
+                        op0=ALU.mult,
+                        op1=ALU.add,
+                        accum_out=(sums[g][:, a : a + 1] if j == TAPS - 1 else None),
+                    )
+
+        def bias_part(m):
+            g, a = divmod(m, GRP)
+            if a == 0:
+                sums[g] = stat_pool.tile([P, GRP], F32, name="sums")
+                ssq[g] = stat_pool.tile([P, GRP], F32, name="ssq")
+            acc[m] = acc_pool.tile([P, D], F32, name="acc")
+            nc.scalar.activation(out=acc[m][:], in_=bvb[:], func=ACT.Copy, scale=csum[:, m : m + 1])
+
+        def residual(m):
+            nc.gpsimd.tensor_tensor(out=acc[m][:], in0=acc[m][:], in1=x_tile(m), op=ALU.add)
+
+        def squares(m):
+            g, a = divmod(m, GRP)
+            junk = junk_pool.tile([P, D], BF16, name="junk")
+            nc.scalar.activation(
+                out=junk[:],
+                in_=acc[m][:],
+                func=ACT.Square,
+                bias=sums[g][:, a : a + 1],
+                scale=-1.0 * D,
+                accum_out=ssq[g][:, a : a + 1],
+            )
+
+        def stats(g):
+            mu[g] = stat_pool.tile([P, GRP], F32, name="mu")
+            nc.gpsimd.tensor_scalar(
+                out=mu[g][:], in0=sums[g][:], scalar1=-1.0 / D, scalar2=0.0, op0=ALU.mult, op1=ALU.add
+            )
+            var = stat_pool.tile([P, GRP], F32, name="var")
+            nc.gpsimd.tensor_scalar(
+                out=var[:], in0=ssq[g][:], scalar1=1.0 / (D * D * D), scalar2=EPS, op0=ALU.mult, op1=ALU.add
+            )
+            rstd[g] = stat_pool.tile([P, GRP], F32, name="rstd")
+            nc.gpsimd.tensor_tensor(out=rstd[g][:], in0=var[:], in1=mhalf[:], op=ALU.pow)
+            nrm[g] = big_pool.tile([P, GRP, D], F32, name="nrm")
+
+        def normalise(m):
+            g, a = divmod(m, GRP)
+            nc.gpsimd.tensor_scalar(
+                out=nrm[g][:, a, :],
+                in0=acc[m][:],
+                scalar1=mu[g][:, a : a + 1],
+                scalar2=rstd[g][:, a : a + 1],
+                op0=ALU.add,
+                op1=ALU.mult,
+            )
+
+        def to_features(g, c):
+            f_ps[c] = psf.tile([P, GRP * P], F32, name="f_ps")
+            for a in range(GRP):
+                nc.tensor.transpose(
+                    out=f_ps[c][:, a * P : (a + 1) * P],
+                    in_=nrm[g][:, a, c * P : (c + 1) * P],
+                    identity=ident_f[:],
+                )
+
+        def affine(g, c):
+            if c == 0:
+                y_t[g] = big_pool.tile([P, GRP, GRP * P], F32, name="y_t")
+            nc.scalar.activation(
+                out=y_t[g][:, c, :],
+                in_=f_ps[c][:],
+                func=ACT.Identity,
+                scale=gb[:, c : c + 1],
+                bias=gb[:, 4 + c : 5 + c],
+            )
+
+        def to_rows(g, a):
+            b_ps[a] = psb.tile([P, D], F32, name="b_ps")
+            for c in range(GRP):
+                nc.tensor.transpose(
+                    out=b_ps[a][:, c * P : (c + 1) * P],
+                    in_=y_t[g][:, c, a * P : (a + 1) * P],
+                    identity=ident_f[:],
+                )
+
+        def leave(g, a):
+            if a == 0:
+                o_sb[g] = out_pool.tile([P, GRP, D], F32, name="o_sb")
+            nc.scalar.copy(out=o_sb[g][:, a, :], in_=b_ps[a][:])
+
+        def store(g):
+            nc.sync.dma_start(out=o_rows[:, GRP * g : GRP * (g + 1), :], in_=o_sb[g][:])
+
+        def stats_one(m):
+            mu[m] = stat_pool.tile([P, 1], F32, name="mu1")
+            g, a = divmod(m, GRP)
+            nc.gpsimd.tensor_scalar(
+                out=mu[m][:], in0=sums[g][:, a : a + 1], scalar1=-1.0 / D, scalar2=0.0, op0=ALU.mult, op1=ALU.add
+            )
+            var = stat_pool.tile([P, 1], F32, name="var1")
+            nc.gpsimd.tensor_scalar(
+                out=var[:],
+                in0=ssq[g][:, a : a + 1],
+                scalar1=1.0 / (D * D * D),
+                scalar2=EPS,
+                op0=ALU.mult,
+                op1=ALU.add,
+            )
+            rstd[m] = stat_pool.tile([P, 1], F32, name="rstd1")
+            nc.gpsimd.tensor_tensor(out=rstd[m][:], in0=var[:], in1=mhalf[:, 0:1], op=ALU.pow)
+
+        def affine_on_vector(m):
+            cen = junk_pool.tile([P, D], F32, name="cen")
+            nc.vector.scalar_tensor_tensor(
+                out=cen[:], in0=acc[m][:], scalar=mu[m][:], in1=gamma_b[:], op0=ALU.add, op1=ALU.mult
+            )
+            o_one = out_pool.tile([P, D], F32, name="o_one")
+            nc.vector.scalar_tensor_tensor(
+                out=o_one[:], in0=cen[:], scalar=rstd[m][:], in1=beta_b[:], op0=ALU.mult, op1=ALU.add
+            )
+            nc.sync.dma_start(out=o_rows[:, m, :], in_=o_one[:])
+
+        NG_T = (RUN - TAIL) // GRP
+
+        for k in range(-4, NT + 4):
+            if 0 <= k + 2 < NT:
+                project(k + 2)
+            g, r = divmod(k - 13, GRP)
+            if r == 0 and 0 <= g - 1 < NG_T:
+                leave(g - 1, 2)
+                leave(g - 1, 3)
+                store(g - 1)
+            if 0 <= g < NG_T:
+                if r == 0:
+                    to_features(g, 0)
+                    to_features(g, 1)
+                if r == 1:
+                    affine(g, 0)
+                    affine(g, 1)
+                    to_features(g, 2)
+                    to_features(g, 3)
+                if r == 2:
+                    affine(g, 2)
+                    affine(g, 3)
+                    to_rows(g, 0)
+                    to_rows(g, 1)
+                if r == 3:
+                    leave(g, 0)
+                    leave(g, 1)
+                    to_rows(g, 2)
+                    to_rows(g, 3)
+            g, r = divmod(k + 7, GRP)
+            if 1 <= g < NG_IN:
+                if r == 0:
+                    turn(g, x_srcs(g), 0, psx, "xt")
+                if r == 1:
+                    regroup(g, 0, nc.scalar.copy)
+                    turn(g, x_srcs(g), 1, psx, "xt")
+                if r == 2:
+                    regroup(g, 1, nc.scalar.copy)
+            if k == 2:
+                gps = psb.tile([P, P], BF16, name="gps", tag="b_ps")
+                nc.tensor.transpose(out=gps[:], in_=gbrow[:], identity=ident_b[:])
+            if 0 <= k - 5 < RUN:
+                squares(k - 5)
+            if 0 <= k + 4 < RUN:
+                bias_part(k + 4)
+            if 0 <= k + 3 < RUN:
+                residual(k + 3)
+            g, r = divmod(k - 9, GRP)
+            if 0 <= g < NG_T:
+                if r == 0:
+                    stats(g)
+                normalise(GRP * g + r)
+            if RUN - TAIL <= k - 6 < RUN:
+                stats_one(k - 6)
+            if 0 <= k < NT:
+                taps(k)
+            if k == 2:
+                nc.vector.tensor_copy(out=gb[:], in_=gps[:, 0:8])
+            if RUN - TAIL <= k - 7 < RUN:
+                affine_on_vector(k - 7)
+            g, r = divmod(k + 4, GRP)
+            if r == 0 and 1 <= g < NG_IN:
+                quantise_x(g)

@@ -16,78 +16,186 @@ AX = mybir.AxisListType
 P = 128
 D = 512
 ROWS = 8192
-RUN = ROWS // P
 TAPS = 5
 NB = 2
 GRP = 4
 EPS = 1e-5
-CHUNKS = [2, 6, 8, 8, 8, 8, 8, 8, 8]
-TAIL = 8
+
+RUN = 40
+TAP_ROWS = RUN * P
+NT = RUN + 2 * NB
+WIN_OUT = P - 2 * NB
+NW = -(-(ROWS - TAP_ROWS) // WIN_OUT)
+BANDW = 130
+NQ = BANDW // TAPS
+
+CHUNKS = [2, 6, 8, 8, 8, 8]
+WIN_CHUNKS = [2, 4, 5, 5, 5, 4]
+TAIL = 5
+LAG = 2
 
 FLOPS = 2 * ROWS * D * D + 2 * ROWS * TAPS * D
+
+
+def win_row0(c):
+    return min(TAP_ROWS + WIN_OUT * c - NB, ROWS - P)
 
 
 def tile_crosssliceattention_pb_t_kernel(tc, x, Wv, bv, attn_band, gamma, beta, out):
     nc = tc.nc
     xf = x.flatten_outer_dims()
-    x_rows = xf.rearrange("(p t) d -> p t d", t=RUN)
-    o_rows = out.flatten_outer_dims().rearrange("(p t) d -> p t d", t=RUN)
+    of = out.flatten_outer_dims()
+    af = attn_band.flatten_outer_dims()
+    a_flat = attn_band.rearrange("b s j -> (b s j)")
+    x_rows = xf[0:TAP_ROWS, :].rearrange("(p t) d -> p t d", t=RUN)
+    o_rows = of[0:TAP_ROWS, :].rearrange("(p t) d -> p t d", t=RUN)
+
+    slots = []
+    given = 0
+    for t in range(NT):
+        slots.append(("tap", t))
+        due = min(NW, max(0, t - 1) * NW // (NT - 3))
+        while given < due:
+            slots.append(("win", given))
+            given += 1
+    NS = len(slots)
+    pos = {}
+    for k in range(NS):
+        pos[slots[k]] = k
+    order = []
+    done = []
+    for k in range(NS + LAG):
+        if k >= LAG and slots[k - LAG][0] == "win":
+            order.append(slots[k - LAG])
+            done.append(k)
+        if k < NS and slots[k][0] == "tap" and slots[k][1] >= 2 * NB:
+            order.append(("tap", slots[k][1] - 2 * NB))
+            done.append(k)
+    NI = len(order)
+    index = {}
+    for n in range(NI):
+        index[order[n]] = n
+    NG_T = (NI - TAIL) // GRP
+    stat_at = {}
+    feat_at = {}
+    last = -100
+    for g in range(NG_T):
+        last = max(done[GRP * g + GRP - 1] + 2, last + GRP)
+        for r in range(GRP):
+            stat_at.setdefault(last + r, []).append((g, r))
+        for r in range(GRP + 1):
+            feat_at.setdefault(last + GRP + r, []).append((g, r))
+    KEND = last + 2 * GRP + 2
+
+    jobs = []
+    for g in range(1, NT // GRP):
+        s0 = pos[("tap", GRP * g)]
+        jobs.append((s0 - 6, "tap", g, 1))
+        jobs.append((s0 - 7, "tap", g, 0))
+    for b in range((NW + 1) // 2):
+        jobs.append((pos[("win", 2 * b)] - 6, "win", b, 0))
+    for b in range((NW + GRP - 1) // GRP):
+        jobs.append((pos[("win", GRP * b)] - 1, "band", b, 0))
+    job_at = {}
+    free = 1000
+    for job in sorted(jobs, reverse=True):
+        free = min(free - 1, job[0])
+        job_at[free] = job
+    KBEG = free
+    quant_at = {}
+    for g in range(1, NT // GRP):
+        quant_at.setdefault(pos[("tap", GRP * g)] - 4, []).append(("tap", g))
+    for b in range((NW + 1) // 2):
+        quant_at.setdefault(pos[("win", 2 * b)] - 4, []).append(("win", b))
 
     with ExitStack() as ctx:
         const = ctx.enter_context(tc.tile_pool(name="const", bufs=1))
         grp_pool = ctx.enter_context(tc.tile_pool(name="grp", bufs=2))
         acc_pool = ctx.enter_context(tc.tile_pool(name="accp", bufs=18))
+        vw_pool = ctx.enter_context(tc.tile_pool(name="vwp", bufs=3))
         junk_pool = ctx.enter_context(tc.tile_pool(name="junkp", bufs=2))
-        stat_pool = ctx.enter_context(tc.tile_pool(name="statp", bufs=5))
+        stat_pool = ctx.enter_context(tc.tile_pool(name="statp", bufs=6))
         big_pool = ctx.enter_context(tc.tile_pool(name="bigp", bufs=2))
         out_pool = ctx.enter_context(tc.tile_pool(name="outp", bufs=3))
         psx = ctx.enter_context(tc.psum_pool(name="psx", bufs=1))
         psv = ctx.enter_context(tc.psum_pool(name="psv", bufs=3))
-        psf = ctx.enter_context(tc.psum_pool(name="psf", bufs=2))
-        psb = ctx.enter_context(tc.psum_pool(name="psb", bufs=2))
+        pso = ctx.enter_context(tc.psum_pool(name="pso", bufs=1))
+        psf = ctx.enter_context(tc.psum_pool(name="psf", bufs=3))
         ctx.enter_context(tc.manual_schedule())
+
+        a_rows = const.tile([P, P * TAPS], BF16, name="a_rows")
+        nc.vector.memset(a_rows[:].bitcast(I32), 0)
+        gbrow = const.tile([P, P], BF16, name="gbrow")
+        nc.vector.memset(gbrow[:].bitcast(I32), 0)
+        halo = const.tile([P, 2 * NB, D], BF16, name="halo")
+        nc.vector.memset(halo[0:1, 0:NB, :].bitcast(I32), 0)
+        mhalf = const.tile([P, GRP], F32, name="mhalf")
+        nc.vector.memset(mhalf[:], -0.5)
 
         w_raw = const.tile([P, GRP, D], BF16, name="w_raw")
         nc.sync.dma_start(out=w_raw[:], in_=Wv.rearrange("(c p) k -> p c k", p=P))
-        halo = const.tile([P, 2 * NB, D], BF16, name="halo")
-        nc.vector.memset(halo[:].bitcast(I32), 0)
         lo_view = xf[RUN - NB : RUN - NB + RUN * (P - 1), :].rearrange("(p t) d -> p t d", t=RUN)
-        hi_view = xf[RUN:ROWS, :].rearrange("(p t) d -> p t d", t=RUN)
+        hi_view = xf[RUN : RUN + TAP_ROWS, :].rearrange("(p t) d -> p t d", t=RUN)
         nc.sync.dma_start(out=halo[1:113, 0:NB, :], in_=lo_view[0:112, 0:NB, :])
         nc.sync.dma_start(out=halo[113:128, 0:NB, :], in_=lo_view[112:127, 0:NB, :])
         x_home = {}
+        x_win = {}
         first = 0
-        for n_tiles in CHUNKS:
-            t = const.tile([P, n_tiles, D], BF16, name="xc%d" % first)
-            nc.sync.dma_start(out=t[:], in_=x_rows[:, first : first + n_tiles, :])
-            for i in range(n_tiles):
-                x_home[first + i] = t[:, i, :]
+        for i in range(len(CHUNKS)):
+            n_tiles = CHUNKS[i]
+            t_x = const.tile([P, n_tiles, D], BF16, name="xc%d" % first)
+            nc.sync.dma_start(out=t_x[:], in_=x_rows[:, first : first + n_tiles, :])
+            for j in range(n_tiles):
+                x_home[first + j] = t_x[:, j, :]
             first += n_tiles
-        nc.sync.dma_start(out=halo[0:112, NB : 2 * NB, :], in_=hi_view[0:112, 0:NB, :])
-        nc.sync.dma_start(out=halo[112:127, NB : 2 * NB, :], in_=hi_view[112:127, 0:NB, :])
+            for j in range(WIN_CHUNKS[i]):
+                c = len(x_win)
+                t_w = const.tile([P, D], BF16, name="xw%d" % c)
+                nc.sync.dma_start(out=t_w[:], in_=xf[win_row0(c) : win_row0(c) + P, :])
+                x_win[c] = t_w[:]
+        nc.sync.dma_start(out=halo[:, NB : 2 * NB, :], in_=hi_view[:, 0:NB, :])
         gamma_b = const.tile([P, D], BF16, name="gamma_b")
         nc.sync.dma_start(out=gamma_b[:], in_=gamma.partition_broadcast(P))
         beta_b = const.tile([P, D], BF16, name="beta_b")
         nc.sync.dma_start(out=beta_b[:], in_=beta.partition_broadcast(P))
 
         a_bf = const.tile([P, RUN * TAPS], BF16, name="a_bf")
-        nc.scalar.dma_start(
-            out=a_bf[:], in_=attn_band.flatten_outer_dims().rearrange("(p t) j -> p (t j)", t=RUN)
-        )
+        nc.scalar.dma_start(out=a_bf[:], in_=af[0:TAP_ROWS, :].rearrange("(p t) j -> p (t j)", t=RUN))
         bvb = const.tile([P, D], BF16, name="bvb")
         nc.scalar.dma_start(out=bvb[:], in_=bv.partition_broadcast(P))
-        gbrow = const.tile([P, P], BF16, name="gbrow")
-        nc.vector.memset(gbrow[:], 0.0)
+        n_even = NW // 2
+        n_odd = n_even - 1
+        step = 2 * TAPS * WIN_OUT
+        for c, n, p0 in ((0, n_even, 0), (1, n_odd, n_even)):
+            a0 = TAPS * win_row0(c)
+            nc.scalar.dma_start(
+                out=a_rows[p0 : p0 + n, :],
+                in_=a_flat[a0 : a0 + n * step].rearrange("(c e) -> c e", e=step)[:, 0 : TAPS * P],
+            )
+        for c in range(NW - 2, NW):
+            nc.scalar.dma_start(
+                out=a_rows[c : c + 1, :],
+                in_=a_flat[TAPS * win_row0(c) : TAPS * (win_row0(c) + P)].rearrange("(c e) -> c e", c=1),
+            )
         nc.scalar.dma_start(out=gbrow[0:4, :], in_=gamma.rearrange("(c p) -> c p", p=P))
         nc.scalar.dma_start(out=gbrow[4:8, :], in_=beta.rearrange("(c p) -> c p", p=P))
 
-        ident_f = const.tile([P, P], F32, name="ident_f")
-        make_identity(nc, ident_f[:])
+        MARGIN = 16
+        wide = const.tile([P, MARGIN + P + MARGIN], F32, name="wide")
+        nc.gpsimd.memset(wide[:, 0:MARGIN], 0.0)
+        nc.gpsimd.memset(wide[:, MARGIN + P :], 0.0)
+        ident_f = wide[:, MARGIN : MARGIN + P]
+        make_identity(nc, ident_f)
         ident_b = const.tile([P, P], BF16, name="ident_b")
         make_identity(nc, ident_b[:])
-
-        mhalf = const.tile([P, GRP], F32, name="mhalf")
-        nc.vector.memset(mhalf[:], -0.5)
+        near = const.tile([P, BANDW], F32, name="near")
+        nc.gpsimd.memset(near[:], 1.0)
+        nc.gpsimd.affine_select(
+            out=near[:], in_=near[:], compare_op=ALU.is_ge, fill=0.0, base=NB, pattern=[[1, BANDW]], channel_multiplier=-1
+        )
+        nc.gpsimd.affine_select(
+            out=near[:], in_=near[:], compare_op=ALU.is_ge, fill=0.0, base=NB, pattern=[[-1, BANDW]], channel_multiplier=1
+        )
 
         def x_tile(i):
             if i < 0:
@@ -100,64 +208,132 @@ def tile_crosssliceattention_pb_t_kernel(tc, x, Wv, bv, attn_band, gamma, beta, 
         nc.vector.tensor_copy(out=a_f[:].rearrange("p t j -> p (t j)"), in_=a_bf[:])
         csum = const.tile([P, RUN], F32, name="csum")
         nc.vector.reduce_sum(out=csum[:], in_=a_f[:], axis=AX.X)
+        turn5 = const.tile([P, TAPS, TAPS], F32, name="turn5")
+        for j in range(TAPS):
+            c0 = MARGIN + NB - j
+            nc.vector.reduce_sum(
+                out=turn5[:, :, j], in_=wide[:, c0 : c0 + BANDW].rearrange("p (q i) -> p i q", i=TAPS), axis=AX.X
+            )
 
         gb = const.tile([P, 8], F32, name="gb")
 
         grouped = {}
-        xt_ps = {}
-
-        def turn(key, srcs, h, pool, tag):
-            xt = pool.tile([P, 2, 2, P], F32, name="xt", tag=tag)
-            for a in range(2):
-                w32 = srcs[2 * h + a].bitcast(F32)
-                for u in range(2):
-                    nc.tensor.transpose(
-                        out=xt[:, a, u, :], in_=w32[:, u : D // 2 : 2], identity=ident_f[:]
-                    )
-            xt_ps[(key, h)] = xt
-
-        def regroup(key, h, engine_copy):
-            if h == 0:
-                grouped[key] = grp_pool.tile([P, GRP * D], BF16, name="grouped", align_bytes=64)
-            g32 = grouped[key][:].bitcast(F32).rearrange("p (a t u) -> p a t u", a=GRP, u=2)
-            engine_copy(
-                out=g32[:, 2 * h : 2 * h + 2, :, :], in_=xt_ps[(key, h)][:].rearrange("p a u t -> p a t u")
-            )
-
-        def quantise(key, codes, scales):
-            nc.vector.quantize_mx(out=codes.bitcast(FP8X4), scales=scales, in_=grouped[key][:])
-
-        w_codes = const.tile([P, D], U32, name="w_codes", align_bytes=64)
-        w_scales = const.tile([P, D], U8, name="w_scales", align_bytes=64)
-        w_srcs = [w_raw[:, c, :] for c in range(GRP)]
-        for h in range(2):
-            turn("w", w_srcs, h, psf, "f_ps")
-        for h in range(2):
-            regroup("w", h, nc.scalar.copy)
-
-        NT = RUN + 2 * NB
-        NG_IN = NT // GRP
-        NG = RUN // GRP
-
-        def x_srcs(g):
-            return [x_tile(GRP * g - NB + a) for a in range(GRP)]
-
         codes = {}
         scales = {}
 
-        def quantise_x(g):
-            codes[g] = grp_pool.tile([P, D], U32, name="codes", align_bytes=64)
-            scales[g] = grp_pool.tile([P, D], U8, name="scales", align_bytes=64)
-            quantise(g, codes[g][:], scales[g][:])
+        def turn(xt, srcs):
+            for a in range(len(srcs)):
+                w32 = srcs[a].bitcast(F32)
+                for u in range(2):
+                    nc.tensor.transpose(out=xt[:, 2 * a + u, :], in_=w32[:, u : D // 2 : 2], identity=ident_f)
 
+        def regroup(dst, xt, n, engine_copy):
+            engine_copy(
+                out=dst.bitcast(F32).rearrange("p (a t u) -> p a t u", a=n, u=2),
+                in_=xt[:, 0 : 2 * n, :].rearrange("p (a u) t -> p a t u", u=2),
+            )
+
+        def quantise(key, n):
+            codes[key] = grp_pool.tile([P, n * P], U32, name="codes", tag="codes%d" % (n > 2), align_bytes=64)
+            scales[key] = grp_pool.tile([P, n * P], U8, name="scales", tag="scales%d" % (n > 2), align_bytes=64)
+            nc.vector.quantize_mx(out=codes[key][:].bitcast(FP8X4), scales=scales[key][:], in_=grouped[key][:])
+
+        def new_grouped(key, n):
+            grouped[key] = grp_pool.tile([P, n * D], BF16, name="grouped", tag="grouped%d" % (n > 2), align_bytes=64)
+
+        w_codes = const.tile([P, D], U32, name="w_codes", align_bytes=64)
+        w_scales = const.tile([P, D], U8, name="w_scales", align_bytes=64)
+        new_grouped("w", GRP)
+        new_grouped(("tap", 0), GRP)
+        wt = [psf.tile([P, GRP, P], F32, name="wt%d" % h, tag="fb") for h in range(2)]
         for h in range(2):
-            turn(0, x_srcs(0), h, psb, "b_ps")
+            turn(wt[h], [w_raw[:, 2 * h + a, :] for a in range(2)])
         for h in range(2):
-            regroup(0, h, nc.vector.tensor_copy)
-        quantise("w", w_codes[:], w_scales[:])
-        quantise_x(0)
+            regroup(grouped["w"][:, 2 * h * D : (2 * h + 2) * D], wt[h], 2, nc.scalar.copy)
+
+        def tap_srcs(g):
+            return [x_tile(GRP * g - NB + a) for a in range(GRP)]
+
+        xt0 = [psv.tile([P, GRP, P], F32, name="xt%d" % h, tag="v_ps") for h in range(2)]
+        for h in range(2):
+            turn(xt0[h], tap_srcs(0)[2 * h : 2 * h + 2])
+        for h in range(2):
+            regroup(grouped[("tap", 0)][:, 2 * h * D : (2 * h + 2) * D], xt0[h], 2, nc.vector.tensor_copy)
+        nc.vector.quantize_mx(out=w_codes[:].bitcast(FP8X4), scales=w_scales[:], in_=grouped["w"][:])
+        quantise(("tap", 0), GRP)
+
+        a_ps = psf.tile([P, TAPS, P], BF16, name="a_ps", tag="fb")
+        for j in range(TAPS):
+            nc.tensor.transpose(out=a_ps[:, j, :], in_=a_rows[:, j : P * TAPS : TAPS], identity=ident_b[:])
+        gps = psf.tile([P, P], BF16, name="gps", tag="fb")
+        nc.tensor.transpose(out=gps[:], in_=gbrow[:], identity=ident_b[:])
+
+        a_win = const.tile([P, NW, TAPS], F32, name="a_win")
+        spread = const.tile([P, NW, TAPS, TAPS], F32, name="spread")
+        a_mod = const.tile([P, NW, TAPS], F32, name="a_mod")
+        band_t = const.tile([P, NW, P], F32, name="band_t")
+
+        def band_weights():
+            for c in range(2):
+                nc.vector.tensor_copy(
+                    out=a_win[:, c : 2 * n_even : 2, :],
+                    in_=a_ps[:, :, c * n_even : (c + 1) * n_even].rearrange("p j c -> p c j"),
+                )
+            nc.vector.tensor_copy(
+                out=a_win[:, NW - 1 : NW, :], in_=a_ps[:, :, NW - 1 : NW].rearrange("p j c -> p c j")
+            )
+            nc.vector.tensor_tensor(
+                out=spread[:],
+                in0=a_win[:].unsqueeze(2).to_broadcast([P, NW, TAPS, TAPS]),
+                in1=turn5[:].unsqueeze(1).to_broadcast([P, NW, TAPS, TAPS]),
+                op=ALU.mult,
+            )
+            nc.vector.reduce_sum(out=a_mod[:], in_=spread[:], axis=AX.X)
+            nc.vector.tensor_copy(out=gb[:], in_=gps[:, 0:8])
+
+        bands = {}
+
+        def band_rows(b):
+            n = min(GRP, NW - GRP * b)
+            bands[b] = grp_pool.tile([P, GRP, BANDW], F32, name="band")
+            nc.gpsimd.tensor_tensor(
+                out=bands[b][:, 0:n, :].rearrange("p w (q i) -> p w q i", i=TAPS),
+                in0=a_mod[:, GRP * b : GRP * b + n, :].unsqueeze(2).to_broadcast([P, n, NQ, TAPS]),
+                in1=near[:].rearrange("p (q i) -> p q i", i=TAPS).unsqueeze(1).to_broadcast([P, n, NQ, TAPS]),
+                op=ALU.mult,
+            )
+
+        banks = {}
+
+        def job_srcs(job):
+            if job[1] == "tap":
+                return tap_srcs(job[2])[2 * job[3] : 2 * job[3] + 2]
+            return [x_win[c] for c in range(2 * job[2], min(NW, 2 * job[2] + 2))]
+
+        def job_turn(job):
+            xt = psx.tile([P, GRP, P], F32, name="xt")
+            banks[job] = xt
+            if job[1] == "band":
+                for w in range(min(GRP, NW - GRP * job[2])):
+                    nc.tensor.transpose(out=xt[:, w, :], in_=bands[job[2]][:, w, 0:P], identity=ident_f)
+            else:
+                turn(xt, job_srcs(job))
+
+        def job_copy(job):
+            xt = banks[job]
+            if job[1] == "band":
+                n = min(GRP, NW - GRP * job[2])
+                nc.scalar.copy(out=band_t[:, GRP * job[2] : GRP * job[2] + n, :], in_=xt[:, 0:n, :])
+                return
+            n = len(job_srcs(job))
+            key = (job[1], job[2])
+            if job[3] == 0:
+                new_grouped(key, GRP if job[1] == "tap" else n)
+            regroup(grouped[key][:, 2 * job[3] * D : (2 * job[3] + n) * D], xt, n, nc.scalar.copy)
 
         v_ps = {}
+        o_ps = {}
+        vw = {}
         acc = {}
         sums = {}
         ssq = {}
@@ -170,74 +346,111 @@ def tile_crosssliceattention_pb_t_kernel(tc, x, Wv, bv, attn_band, gamma, beta, 
         b_ps = {}
 
         def project(k):
-            g, a = divmod(k, GRP)
+            kind, i = slots[k]
+            key, a = (("tap", i // GRP), i % GRP) if kind == "tap" else (("win", i // 2), i % 2)
             v_ps[k] = psv.tile([P, D], F32, name="v_ps")
             nc.tensor.matmul_mx(
                 out=v_ps[k][:],
-                lhsT=codes[g][:, a * P : (a + 1) * P].bitcast(FP8X4),
-                lhsT_scale=scales[g][:, a * P : (a + 1) * P],
+                lhsT=codes[key][:, a * P : (a + 1) * P].bitcast(FP8X4),
+                lhsT_scale=scales[key][:, a * P : (a + 1) * P],
                 rhs=w_codes[:].bitcast(FP8X4),
                 rhs_scale=w_scales[:],
                 start=True,
                 stop=True,
             )
 
+        def sum_place(n):
+            g, a = divmod(n, GRP)
+            if g not in sums:
+                sums[g] = stat_pool.tile([P, GRP], F32, name="sums")
+                ssq[g] = stat_pool.tile([P, GRP], F32, name="ssq")
+            return sums[g][:, a : a + 1]
+
         def taps(k):
+            t = slots[k][1]
             for j in range(TAPS - 1, -1, -1):
-                m = k - j
+                m = t - j
                 if 0 <= m < RUN:
-                    g, a = divmod(m, GRP)
+                    n = index[("tap", m)]
                     nc.vector.scalar_tensor_tensor(
-                        out=acc[m][:],
+                        out=acc[n][:],
                         in0=v_ps[k][:],
                         scalar=a_f[:, m, j : j + 1],
-                        in1=acc[m][:],
+                        in1=acc[n][:],
                         op0=ALU.mult,
                         op1=ALU.add,
-                        accum_out=(sums[g][:, a : a + 1] if j == TAPS - 1 else None),
+                        accum_out=(sum_place(n) if j == TAPS - 1 else None),
                     )
 
         def bias_part(m):
-            g, a = divmod(m, GRP)
-            if a == 0:
-                sums[g] = stat_pool.tile([P, GRP], F32, name="sums")
-                ssq[g] = stat_pool.tile([P, GRP], F32, name="ssq")
-            acc[m] = acc_pool.tile([P, D], F32, name="acc")
-            nc.scalar.activation(out=acc[m][:], in_=bvb[:], func=ACT.Copy, scale=csum[:, m : m + 1])
+            n = index[("tap", m)]
+            acc[n] = acc_pool.tile([P, D], F32, name="acc")
+            if m % 2 == 0:
+                nc.scalar.activation(out=acc[n][:], in_=bvb[:], func=ACT.Copy, scale=csum[:, m : m + 1])
+            else:
+                nc.gpsimd.tensor_scalar(
+                    out=acc[n][:], in0=bvb[:], scalar1=csum[:, m : m + 1], scalar2=0.0, op0=ALU.mult, op1=ALU.add
+                )
 
         def residual(m):
-            nc.gpsimd.tensor_tensor(out=acc[m][:], in0=acc[m][:], in1=x_tile(m), op=ALU.add)
+            n = index[("tap", m)]
+            nc.gpsimd.tensor_tensor(out=acc[n][:], in0=acc[n][:], in1=x_tile(m), op=ALU.add)
 
-        def squares(m):
-            g, a = divmod(m, GRP)
+        def win_leave(k):
+            c = slots[k][1]
+            vw[c] = vw_pool.tile([P, D], F32, name="vw")
+            nc.vector.tensor_tensor(out=vw[c][:], in0=v_ps[k][:], in1=bvb[:], op=ALU.add)
+
+        def win_mix(c):
+            o_ps[c] = pso.tile([P, D], F32, name="o_ps")
+            nc.tensor.matmul(out=o_ps[c][:], lhsT=band_t[:, c, :], rhs=vw[c][:], start=True, stop=True)
+
+        def win_residual(c):
+            n = index[("win", c)]
+            acc[n] = acc_pool.tile([P, D], F32, name="acc")
+            nc.vector.scalar_tensor_tensor(
+                out=acc[n][:],
+                in0=o_ps[c][:],
+                scalar=1.0,
+                in1=x_win[c],
+                op0=ALU.mult,
+                op1=ALU.add,
+                accum_out=sum_place(n),
+            )
+
+        def squares(n):
+            g, a = divmod(n, GRP)
             junk = junk_pool.tile([P, D], BF16, name="junk")
             nc.scalar.activation(
                 out=junk[:],
-                in_=acc[m][:],
+                in_=acc[n][:],
                 func=ACT.Square,
                 bias=sums[g][:, a : a + 1],
                 scale=-1.0 * D,
                 accum_out=ssq[g][:, a : a + 1],
             )
 
-        def stats(g):
-            mu[g] = stat_pool.tile([P, GRP], F32, name="mu")
+        def stats(key, s, q, width):
+            mu[key] = stat_pool.tile([P, GRP], F32, name="mu")
             nc.gpsimd.tensor_scalar(
-                out=mu[g][:], in0=sums[g][:], scalar1=-1.0 / D, scalar2=0.0, op0=ALU.mult, op1=ALU.add
+                out=mu[key][:, 0:width], in0=s, scalar1=-1.0 / D, scalar2=0.0, op0=ALU.mult, op1=ALU.add
             )
             var = stat_pool.tile([P, GRP], F32, name="var")
             nc.gpsimd.tensor_scalar(
-                out=var[:], in0=ssq[g][:], scalar1=1.0 / (D * D * D), scalar2=EPS, op0=ALU.mult, op1=ALU.add
+                out=var[:, 0:width], in0=q, scalar1=1.0 / (D * D * D), scalar2=EPS, op0=ALU.mult, op1=ALU.add
             )
-            rstd[g] = stat_pool.tile([P, GRP], F32, name="rstd")
-            nc.gpsimd.tensor_tensor(out=rstd[g][:], in0=var[:], in1=mhalf[:], op=ALU.pow)
-            nrm[g] = big_pool.tile([P, GRP, D], F32, name="nrm")
+            rstd[key] = stat_pool.tile([P, GRP], F32, name="rstd")
+            nc.gpsimd.tensor_tensor(
+                out=rstd[key][:, 0:width], in0=var[:, 0:width], in1=mhalf[:, 0:width], op=ALU.pow
+            )
 
-        def normalise(m):
-            g, a = divmod(m, GRP)
+        def normalise(n):
+            g, a = divmod(n, GRP)
+            if a == 0:
+                nrm[g] = big_pool.tile([P, GRP, D], F32, name="nrm")
             nc.gpsimd.tensor_scalar(
                 out=nrm[g][:, a, :],
-                in0=acc[m][:],
+                in0=acc[n][:],
                 scalar1=mu[g][:, a : a + 1],
                 scalar2=rstd[g][:, a : a + 1],
                 op0=ALU.add,
@@ -245,12 +458,10 @@ def tile_crosssliceattention_pb_t_kernel(tc, x, Wv, bv, attn_band, gamma, beta, 
             )
 
         def to_features(g, c):
-            f_ps[c] = psf.tile([P, GRP * P], F32, name="f_ps")
+            f_ps[c] = psf.tile([P, GRP * P], F32, name="f_ps", tag="fb")
             for a in range(GRP):
                 nc.tensor.transpose(
-                    out=f_ps[c][:, a * P : (a + 1) * P],
-                    in_=nrm[g][:, a, c * P : (c + 1) * P],
-                    identity=ident_f[:],
+                    out=f_ps[c][:, a * P : (a + 1) * P], in_=nrm[g][:, a, c * P : (c + 1) * P], identity=ident_f
                 )
 
         def affine(g, c):
@@ -265,62 +476,45 @@ def tile_crosssliceattention_pb_t_kernel(tc, x, Wv, bv, attn_band, gamma, beta, 
             )
 
         def to_rows(g, a):
-            b_ps[a] = psb.tile([P, D], F32, name="b_ps")
+            b_ps[a] = psf.tile([P, D], F32, name="b_ps", tag="fb")
             for c in range(GRP):
                 nc.tensor.transpose(
-                    out=b_ps[a][:, c * P : (c + 1) * P],
-                    in_=y_t[g][:, c, a * P : (a + 1) * P],
-                    identity=ident_f[:],
+                    out=b_ps[a][:, c * P : (c + 1) * P], in_=y_t[g][:, c, a * P : (a + 1) * P], identity=ident_f
                 )
+
+        def store(n, tile):
+            kind, i = order[n]
+            if kind == "tap":
+                nc.sync.dma_start(out=o_rows[:, i, :], in_=tile)
+            else:
+                r0 = TAP_ROWS + WIN_OUT * i
+                rows = min(WIN_OUT, ROWS - r0)
+                p0 = r0 - win_row0(i)
+                nc.sync.dma_start(out=of[r0 : r0 + rows, :], in_=tile[p0 : p0 + rows, :])
 
         def leave(g, a):
             if a == 0:
                 o_sb[g] = out_pool.tile([P, GRP, D], F32, name="o_sb")
             nc.scalar.copy(out=o_sb[g][:, a, :], in_=b_ps[a][:])
+            store(GRP * g + a, o_sb[g][:, a, :])
 
-        def store(g):
-            nc.sync.dma_start(out=o_rows[:, GRP * g : GRP * (g + 1), :], in_=o_sb[g][:])
-
-        def stats_one(m):
-            mu[m] = stat_pool.tile([P, 1], F32, name="mu1")
-            g, a = divmod(m, GRP)
-            nc.gpsimd.tensor_scalar(
-                out=mu[m][:], in0=sums[g][:, a : a + 1], scalar1=-1.0 / D, scalar2=0.0, op0=ALU.mult, op1=ALU.add
-            )
-            var = stat_pool.tile([P, 1], F32, name="var1")
-            nc.gpsimd.tensor_scalar(
-                out=var[:],
-                in0=ssq[g][:, a : a + 1],
-                scalar1=1.0 / (D * D * D),
-                scalar2=EPS,
-                op0=ALU.mult,
-                op1=ALU.add,
-            )
-            rstd[m] = stat_pool.tile([P, 1], F32, name="rstd1")
-            nc.gpsimd.tensor_tensor(out=rstd[m][:], in0=var[:], in1=mhalf[:, 0:1], op=ALU.pow)
-
-        def affine_on_vector(m):
+        def affine_on_vector(n):
             cen = junk_pool.tile([P, D], F32, name="cen")
             nc.vector.scalar_tensor_tensor(
-                out=cen[:], in0=acc[m][:], scalar=mu[m][:], in1=gamma_b[:], op0=ALU.add, op1=ALU.mult
+                out=cen[:], in0=acc[n][:], scalar=mu[("one", n)][:, 0:1], in1=gamma_b[:], op0=ALU.add, op1=ALU.mult
             )
             o_one = out_pool.tile([P, D], F32, name="o_one")
             nc.vector.scalar_tensor_tensor(
-                out=o_one[:], in0=cen[:], scalar=rstd[m][:], in1=beta_b[:], op0=ALU.mult, op1=ALU.add
+                out=o_one[:], in0=cen[:], scalar=rstd[("one", n)][:, 0:1], in1=beta_b[:], op0=ALU.mult, op1=ALU.add
             )
-            nc.sync.dma_start(out=o_rows[:, m, :], in_=o_one[:])
+            store(n, o_one[:])
 
-        NG_T = (RUN - TAIL) // GRP
-
-        for k in range(-4, NT + 4):
-            if 0 <= k + 2 < NT:
+        for k in range(min(KBEG, -4), max(KEND, NS + LAG + 4)):
+            if 0 <= k + 2 < NS:
                 project(k + 2)
-            g, r = divmod(k - 13, GRP)
-            if r == 0 and 0 <= g - 1 < NG_T:
-                leave(g - 1, 2)
-                leave(g - 1, 3)
-                store(g - 1)
-            if 0 <= g < NG_T:
+            if 0 <= k - 1 < NS and slots[k - 1][0] == "win":
+                win_mix(slots[k - 1][1])
+            for g, r in feat_at.get(k, []):
                 if r == 0:
                     to_features(g, 0)
                     to_features(g, 1)
@@ -339,37 +533,41 @@ def tile_crosssliceattention_pb_t_kernel(tc, x, Wv, bv, attn_band, gamma, beta, 
                     leave(g, 1)
                     to_rows(g, 2)
                     to_rows(g, 3)
-            g, r = divmod(k + 7, GRP)
-            if 1 <= g < NG_IN:
+                if r == 4:
+                    leave(g, 2)
+                    leave(g, 3)
+            if k - 1 in job_at:
+                job_copy(job_at[k - 1])
+            if k in job_at:
+                job_turn(job_at[k])
+            for n in range(NI):
+                if done[n] == k - 1:
+                    squares(n)
+            if 0 <= k + 4 < NS and slots[k + 4][0] == "tap" and slots[k + 4][1] < RUN:
+                bias_part(slots[k + 4][1])
+            if 0 <= k + 3 < NS and slots[k + 3][0] == "tap" and slots[k + 3][1] < RUN:
+                residual(slots[k + 3][1])
+            if k + 1 in job_at and job_at[k + 1][1] == "band":
+                band_rows(job_at[k + 1][2])
+            for g, r in stat_at.get(k, []):
                 if r == 0:
-                    turn(g, x_srcs(g), 0, psx, "xt")
-                if r == 1:
-                    regroup(g, 0, nc.scalar.copy)
-                    turn(g, x_srcs(g), 1, psx, "xt")
-                if r == 2:
-                    regroup(g, 1, nc.scalar.copy)
-            if k == 2:
-                gps = psb.tile([P, P], BF16, name="gps", tag="b_ps")
-                nc.tensor.transpose(out=gps[:], in_=gbrow[:], identity=ident_b[:])
-            if 0 <= k - 5 < RUN:
-                squares(k - 5)
-            if 0 <= k + 4 < RUN:
-                bias_part(k + 4)
-            if 0 <= k + 3 < RUN:
-                residual(k + 3)
-            g, r = divmod(k - 9, GRP)
-            if 0 <= g < NG_T:
-                if r == 0:
-                    stats(g)
+                    stats(g, sums[g][:], ssq[g][:], GRP)
                 normalise(GRP * g + r)
-            if RUN - TAIL <= k - 6 < RUN:
-                stats_one(k - 6)
-            if 0 <= k < NT:
-                taps(k)
-            if k == 2:
-                nc.vector.tensor_copy(out=gb[:], in_=gps[:, 0:8])
-            if RUN - TAIL <= k - 7 < RUN:
-                affine_on_vector(k - 7)
-            g, r = divmod(k + 4, GRP)
-            if r == 0 and 1 <= g < NG_IN:
-                quantise_x(g)
+            for n in range(GRP * NG_T, NI):
+                if done[n] == k - 2:
+                    g, a = divmod(n, GRP)
+                    stats(("one", n), sums[g][:, a : a + 1], ssq[g][:, a : a + 1], 1)
+            if LAG <= k < NS + LAG and slots[k - LAG][0] == "win":
+                win_residual(slots[k - LAG][1])
+            if 0 <= k < NS:
+                if slots[k][0] == "tap":
+                    taps(k)
+                else:
+                    win_leave(k)
+            if k == 0:
+                band_weights()
+            for n in range(GRP * NG_T, NI):
+                if done[n] == k - 3:
+                    affine_on_vector(n)
+            for key in quant_at.get(k, []):
+                quantise(key, GRP if key[0] == "tap" else min(2, NW - 2 * key[1]))

from contextlib import ExitStack

import concourse.mybir as mybir
from concourse.masks import make_identity

F32 = mybir.dt.float32
BF16 = mybir.dt.bfloat16
U32 = mybir.dt.uint32
U8 = mybir.dt.uint8
I32 = mybir.dt.int32
FP8X4 = mybir.dt.float8_e4m3fn_x4
ALU = mybir.AluOpType
ACT = mybir.ActivationFunctionType
AX = mybir.AxisListType

P = 128
D = 512
ROWS = 8192
TAPS = 5
NB = 2
GRP = 4
EPS = 1e-5

RUN = 40
TAP_ROWS = RUN * P
NT = RUN + 2 * NB
WIN_OUT = P - 2 * NB
NW = -(-(ROWS - TAP_ROWS) // WIN_OUT)
BANDW = 130
NQ = BANDW // TAPS

CHUNKS = [2, 6, 8, 8, 8, 8]
WIN_CHUNKS = [2, 4, 5, 5, 5, 4]
TAIL = 5
LAG = 2

FLOPS = 2 * ROWS * D * D + 2 * ROWS * TAPS * D


def win_row0(c):
    return min(TAP_ROWS + WIN_OUT * c - NB, ROWS - P)


def tile_crosssliceattention_pb_t_kernel(tc, x, Wv, bv, attn_band, gamma, beta, out):
    nc = tc.nc
    xf = x.flatten_outer_dims()
    of = out.flatten_outer_dims()
    af = attn_band.flatten_outer_dims()
    a_flat = attn_band.rearrange("b s j -> (b s j)")
    x_rows = xf[0:TAP_ROWS, :].rearrange("(p t) d -> p t d", t=RUN)
    o_rows = of[0:TAP_ROWS, :].rearrange("(p t) d -> p t d", t=RUN)

    slots = []
    given = 0
    for t in range(NT):
        slots.append(("tap", t))
        due = min(NW, max(0, t - 1) * NW // (NT - 3))
        while given < due:
            slots.append(("win", given))
            given += 1
    NS = len(slots)
    pos = {}
    for k in range(NS):
        pos[slots[k]] = k
    order = []
    done = []
    for k in range(NS + LAG):
        if k >= LAG and slots[k - LAG][0] == "win":
            order.append(slots[k - LAG])
            done.append(k)
        if k < NS and slots[k][0] == "tap" and slots[k][1] >= 2 * NB:
            order.append(("tap", slots[k][1] - 2 * NB))
            done.append(k)
    NI = len(order)
    index = {}
    for n in range(NI):
        index[order[n]] = n
    NG_T = (NI - TAIL) // GRP
    stat_at = {}
    feat_at = {}
    last = -100
    for g in range(NG_T):
        last = max(done[GRP * g + GRP - 1] + 2, last + GRP)
        for r in range(GRP):
            stat_at.setdefault(last + r, []).append((g, r))
        for r in range(GRP + 1):
            feat_at.setdefault(last + GRP + r, []).append((g, r))
    KEND = last + 2 * GRP + 2

    jobs = []
    for g in range(1, NT // GRP):
        s0 = pos[("tap", GRP * g)]
        jobs.append((s0 - 6, "tap", g, 1))
        jobs.append((s0 - 7, "tap", g, 0))
    for b in range((NW + 1) // 2):
        jobs.append((pos[("win", 2 * b)] - 6, "win", b, 0))
    for b in range((NW + GRP - 1) // GRP):
        jobs.append((pos[("win", GRP * b)] - 1, "band", b, 0))
    job_at = {}
    free = 1000
    for job in sorted(jobs, reverse=True):
        free = min(free - 1, job[0])
        job_at[free] = job
    KBEG = free
    quant_at = {}
    for g in range(1, NT // GRP):
        quant_at.setdefault(pos[("tap", GRP * g)] - 4, []).append(("tap", g))
    for b in range((NW + 1) // 2):
        quant_at.setdefault(pos[("win", 2 * b)] - 4, []).append(("win", b))

    with ExitStack() as ctx:
        const = ctx.enter_context(tc.tile_pool(name="const", bufs=1))
        grp_pool = ctx.enter_context(tc.tile_pool(name="grp", bufs=2))
        acc_pool = ctx.enter_context(tc.tile_pool(name="accp", bufs=18))
        vw_pool = ctx.enter_context(tc.tile_pool(name="vwp", bufs=3))
        junk_pool = ctx.enter_context(tc.tile_pool(name="junkp", bufs=2))
        stat_pool = ctx.enter_context(tc.tile_pool(name="statp", bufs=6))
        big_pool = ctx.enter_context(tc.tile_pool(name="bigp", bufs=2))
        out_pool = ctx.enter_context(tc.tile_pool(name="outp", bufs=3))
        psx = ctx.enter_context(tc.psum_pool(name="psx", bufs=1))
        psv = ctx.enter_context(tc.psum_pool(name="psv", bufs=3))
        pso = ctx.enter_context(tc.psum_pool(name="pso", bufs=1))
        psf = ctx.enter_context(tc.psum_pool(name="psf", bufs=3))
        ctx.enter_context(tc.manual_schedule())

        a_rows = const.tile([P, P * TAPS], BF16, name="a_rows")
        nc.vector.memset(a_rows[:].bitcast(I32), 0)
        gbrow = const.tile([P, P], BF16, name="gbrow")
        nc.vector.memset(gbrow[:].bitcast(I32), 0)
        halo = const.tile([P, 2 * NB, D], BF16, name="halo")
        nc.vector.memset(halo[0:1, 0:NB, :].bitcast(I32), 0)
        mhalf = const.tile([P, GRP], F32, name="mhalf")
        nc.vector.memset(mhalf[:], -0.5)

        w_raw = const.tile([P, GRP, D], BF16, name="w_raw")
        nc.sync.dma_start(out=w_raw[:], in_=Wv.rearrange("(c p) k -> p c k", p=P))
        lo_view = xf[RUN - NB : RUN - NB + RUN * (P - 1), :].rearrange("(p t) d -> p t d", t=RUN)
        hi_view = xf[RUN : RUN + TAP_ROWS, :].rearrange("(p t) d -> p t d", t=RUN)
        nc.sync.dma_start(out=halo[1:113, 0:NB, :], in_=lo_view[0:112, 0:NB, :])
        nc.sync.dma_start(out=halo[113:128, 0:NB, :], in_=lo_view[112:127, 0:NB, :])
        x_home = {}
        x_win = {}
        first = 0
        for i in range(len(CHUNKS)):
            n_tiles = CHUNKS[i]
            t_x = const.tile([P, n_tiles, D], BF16, name="xc%d" % first)
            nc.sync.dma_start(out=t_x[:], in_=x_rows[:, first : first + n_tiles, :])
            for j in range(n_tiles):
                x_home[first + j] = t_x[:, j, :]
            first += n_tiles
            for j in range(WIN_CHUNKS[i]):
                c = len(x_win)
                t_w = const.tile([P, D], BF16, name="xw%d" % c)
                nc.sync.dma_start(out=t_w[:], in_=xf[win_row0(c) : win_row0(c) + P, :])
                x_win[c] = t_w[:]
        nc.sync.dma_start(out=halo[:, NB : 2 * NB, :], in_=hi_view[:, 0:NB, :])
        gamma_b = const.tile([P, D], BF16, name="gamma_b")
        nc.sync.dma_start(out=gamma_b[:], in_=gamma.partition_broadcast(P))
        beta_b = const.tile([P, D], BF16, name="beta_b")
        nc.sync.dma_start(out=beta_b[:], in_=beta.partition_broadcast(P))

        a_bf = const.tile([P, RUN * TAPS], BF16, name="a_bf")
        nc.scalar.dma_start(out=a_bf[:], in_=af[0:TAP_ROWS, :].rearrange("(p t) j -> p (t j)", t=RUN))
        bvb = const.tile([P, D], BF16, name="bvb")
        nc.scalar.dma_start(out=bvb[:], in_=bv.partition_broadcast(P))
        n_even = NW // 2
        n_odd = n_even - 1
        step = 2 * TAPS * WIN_OUT
        for c, n, p0 in ((0, n_even, 0), (1, n_odd, n_even)):
            a0 = TAPS * win_row0(c)
            nc.scalar.dma_start(
                out=a_rows[p0 : p0 + n, :],
                in_=a_flat[a0 : a0 + n * step].rearrange("(c e) -> c e", e=step)[:, 0 : TAPS * P],
            )
        for c in range(NW - 2, NW):
            nc.scalar.dma_start(
                out=a_rows[c : c + 1, :],
                in_=a_flat[TAPS * win_row0(c) : TAPS * (win_row0(c) + P)].rearrange("(c e) -> c e", c=1),
            )
        nc.scalar.dma_start(out=gbrow[0:4, :], in_=gamma.rearrange("(c p) -> c p", p=P))
        nc.scalar.dma_start(out=gbrow[4:8, :], in_=beta.rearrange("(c p) -> c p", p=P))

        MARGIN = 16
        wide = const.tile([P, MARGIN + P + MARGIN], F32, name="wide")
        nc.gpsimd.memset(wide[:, 0:MARGIN], 0.0)
        nc.gpsimd.memset(wide[:, MARGIN + P :], 0.0)
        ident_f = wide[:, MARGIN : MARGIN + P]
        make_identity(nc, ident_f)
        ident_b = const.tile([P, P], BF16, name="ident_b")
        make_identity(nc, ident_b[:])
        near = const.tile([P, BANDW], F32, name="near")
        nc.gpsimd.memset(near[:], 1.0)
        nc.gpsimd.affine_select(
            out=near[:], in_=near[:], compare_op=ALU.is_ge, fill=0.0, base=NB, pattern=[[1, BANDW]], channel_multiplier=-1
        )
        nc.gpsimd.affine_select(
            out=near[:], in_=near[:], compare_op=ALU.is_ge, fill=0.0, base=NB, pattern=[[-1, BANDW]], channel_multiplier=1
        )

        def x_tile(i):
            if i < 0:
                return halo[:, i + NB, :]
            if i >= RUN:
                return halo[:, i - RUN + NB, :]
            return x_home[i]

        a_f = const.tile([P, RUN, TAPS], F32, name="a_f")
        nc.vector.tensor_copy(out=a_f[:].rearrange("p t j -> p (t j)"), in_=a_bf[:])
        csum = const.tile([P, RUN], F32, name="csum")
        nc.vector.reduce_sum(out=csum[:], in_=a_f[:], axis=AX.X)
        turn5 = const.tile([P, TAPS, TAPS], F32, name="turn5")
        for j in range(TAPS):
            c0 = MARGIN + NB - j
            nc.vector.reduce_sum(
                out=turn5[:, :, j], in_=wide[:, c0 : c0 + BANDW].rearrange("p (q i) -> p i q", i=TAPS), axis=AX.X
            )

        gb = const.tile([P, 8], F32, name="gb")

        grouped = {}
        codes = {}
        scales = {}

        def turn(xt, srcs):
            for a in range(len(srcs)):
                w32 = srcs[a].bitcast(F32)
                for u in range(2):
                    nc.tensor.transpose(out=xt[:, 2 * a + u, :], in_=w32[:, u : D // 2 : 2], identity=ident_f)

        def regroup(dst, xt, n, engine_copy):
            engine_copy(
                out=dst.bitcast(F32).rearrange("p (a t u) -> p a t u", a=n, u=2),
                in_=xt[:, 0 : 2 * n, :].rearrange("p (a u) t -> p a t u", u=2),
            )

        def quantise(key, n):
            codes[key] = grp_pool.tile([P, n * P], U32, name="codes", tag="codes%d" % (n > 2), align_bytes=64)
            scales[key] = grp_pool.tile([P, n * P], U8, name="scales", tag="scales%d" % (n > 2), align_bytes=64)
            nc.vector.quantize_mx(out=codes[key][:].bitcast(FP8X4), scales=scales[key][:], in_=grouped[key][:])

        def new_grouped(key, n):
            grouped[key] = grp_pool.tile([P, n * D], BF16, name="grouped", tag="grouped%d" % (n > 2), align_bytes=64)

        w_codes = const.tile([P, D], U32, name="w_codes", align_bytes=64)
        w_scales = const.tile([P, D], U8, name="w_scales", align_bytes=64)
        new_grouped("w", GRP)
        new_grouped(("tap", 0), GRP)
        wt = [psf.tile([P, GRP, P], F32, name="wt%d" % h, tag="fb") for h in range(2)]
        for h in range(2):
            turn(wt[h], [w_raw[:, 2 * h + a, :] for a in range(2)])
        for h in range(2):
            regroup(grouped["w"][:, 2 * h * D : (2 * h + 2) * D], wt[h], 2, nc.scalar.copy)

        def tap_srcs(g):
            return [x_tile(GRP * g - NB + a) for a in range(GRP)]

        xt0 = [psv.tile([P, GRP, P], F32, name="xt%d" % h, tag="v_ps") for h in range(2)]
        for h in range(2):
            turn(xt0[h], tap_srcs(0)[2 * h : 2 * h + 2])
        for h in range(2):
            regroup(grouped[("tap", 0)][:, 2 * h * D : (2 * h + 2) * D], xt0[h], 2, nc.vector.tensor_copy)
        nc.vector.quantize_mx(out=w_codes[:].bitcast(FP8X4), scales=w_scales[:], in_=grouped["w"][:])
        quantise(("tap", 0), GRP)

        a_ps = psf.tile([P, TAPS, P], BF16, name="a_ps", tag="fb")
        for j in range(TAPS):
            nc.tensor.transpose(out=a_ps[:, j, :], in_=a_rows[:, j : P * TAPS : TAPS], identity=ident_b[:])
        gps = psf.tile([P, P], BF16, name="gps", tag="fb")
        nc.tensor.transpose(out=gps[:], in_=gbrow[:], identity=ident_b[:])

        a_win = const.tile([P, NW, TAPS], F32, name="a_win")
        spread = const.tile([P, NW, TAPS, TAPS], F32, name="spread")
        a_mod = const.tile([P, NW, TAPS], F32, name="a_mod")
        band_t = const.tile([P, NW, P], F32, name="band_t")

        def band_weights():
            for c in range(2):
                nc.vector.tensor_copy(
                    out=a_win[:, c : 2 * n_even : 2, :],
                    in_=a_ps[:, :, c * n_even : (c + 1) * n_even].rearrange("p j c -> p c j"),
                )
            nc.vector.tensor_copy(
                out=a_win[:, NW - 1 : NW, :], in_=a_ps[:, :, NW - 1 : NW].rearrange("p j c -> p c j")
            )
            nc.vector.tensor_tensor(
                out=spread[:],
                in0=a_win[:].unsqueeze(2).to_broadcast([P, NW, TAPS, TAPS]),
                in1=turn5[:].unsqueeze(1).to_broadcast([P, NW, TAPS, TAPS]),
                op=ALU.mult,
            )
            nc.vector.reduce_sum(out=a_mod[:], in_=spread[:], axis=AX.X)
            nc.vector.tensor_copy(out=gb[:], in_=gps[:, 0:8])

        bands = {}

        def band_rows(b):
            n = min(GRP, NW - GRP * b)
            bands[b] = grp_pool.tile([P, GRP, BANDW], F32, name="band")
            nc.gpsimd.tensor_tensor(
                out=bands[b][:, 0:n, :].rearrange("p w (q i) -> p w q i", i=TAPS),
                in0=a_mod[:, GRP * b : GRP * b + n, :].unsqueeze(2).to_broadcast([P, n, NQ, TAPS]),
                in1=near[:].rearrange("p (q i) -> p q i", i=TAPS).unsqueeze(1).to_broadcast([P, n, NQ, TAPS]),
                op=ALU.mult,
            )

        banks = {}

        def job_srcs(job):
            if job[1] == "tap":
                return tap_srcs(job[2])[2 * job[3] : 2 * job[3] + 2]
            return [x_win[c] for c in range(2 * job[2], min(NW, 2 * job[2] + 2))]

        def job_turn(job):
            xt = psx.tile([P, GRP, P], F32, name="xt")
            banks[job] = xt
            if job[1] == "band":
                for w in range(min(GRP, NW - GRP * job[2])):
                    nc.tensor.transpose(out=xt[:, w, :], in_=bands[job[2]][:, w, 0:P], identity=ident_f)
            else:
                turn(xt, job_srcs(job))

        def job_copy(job):
            xt = banks[job]
            if job[1] == "band":
                n = min(GRP, NW - GRP * job[2])
                nc.scalar.copy(out=band_t[:, GRP * job[2] : GRP * job[2] + n, :], in_=xt[:, 0:n, :])
                return
            n = len(job_srcs(job))
            key = (job[1], job[2])
            if job[3] == 0:
                new_grouped(key, GRP if job[1] == "tap" else n)
            regroup(grouped[key][:, 2 * job[3] * D : (2 * job[3] + n) * D], xt, n, nc.scalar.copy)

        v_ps = {}
        o_ps = {}
        vw = {}
        acc = {}
        sums = {}
        ssq = {}
        mu = {}
        rstd = {}
        nrm = {}
        y_t = {}
        o_sb = {}
        f_ps = {}
        b_ps = {}

        def project(k):
            kind, i = slots[k]
            key, a = (("tap", i // GRP), i % GRP) if kind == "tap" else (("win", i // 2), i % 2)
            v_ps[k] = psv.tile([P, D], F32, name="v_ps")
            nc.tensor.matmul_mx(
                out=v_ps[k][:],
                lhsT=codes[key][:, a * P : (a + 1) * P].bitcast(FP8X4),
                lhsT_scale=scales[key][:, a * P : (a + 1) * P],
                rhs=w_codes[:].bitcast(FP8X4),
                rhs_scale=w_scales[:],
                start=True,
                stop=True,
            )

        def sum_place(n):
            g, a = divmod(n, GRP)
            if g not in sums:
                sums[g] = stat_pool.tile([P, GRP], F32, name="sums")
                ssq[g] = stat_pool.tile([P, GRP], F32, name="ssq")
            return sums[g][:, a : a + 1]

        def taps(k):
            t = slots[k][1]
            for j in range(TAPS - 1, -1, -1):
                m = t - j
                if 0 <= m < RUN:
                    n = index[("tap", m)]
                    nc.vector.scalar_tensor_tensor(
                        out=acc[n][:],
                        in0=v_ps[k][:],
                        scalar=a_f[:, m, j : j + 1],
                        in1=acc[n][:],
                        op0=ALU.mult,
                        op1=ALU.add,
                        accum_out=(sum_place(n) if j == TAPS - 1 else None),
                    )

        def bias_part(m):
            n = index[("tap", m)]
            acc[n] = acc_pool.tile([P, D], F32, name="acc")
            if m % 2 == 0:
                nc.scalar.activation(out=acc[n][:], in_=bvb[:], func=ACT.Copy, scale=csum[:, m : m + 1])
            else:
                nc.gpsimd.tensor_scalar(
                    out=acc[n][:], in0=bvb[:], scalar1=csum[:, m : m + 1], scalar2=0.0, op0=ALU.mult, op1=ALU.add
                )

        def residual(m):
            n = index[("tap", m)]
            nc.gpsimd.tensor_tensor(out=acc[n][:], in0=acc[n][:], in1=x_tile(m), op=ALU.add)

        def win_leave(k):
            c = slots[k][1]
            vw[c] = vw_pool.tile([P, D], F32, name="vw")
            nc.vector.tensor_tensor(out=vw[c][:], in0=v_ps[k][:], in1=bvb[:], op=ALU.add)

        def win_mix(c):
            o_ps[c] = pso.tile([P, D], F32, name="o_ps")
            nc.tensor.matmul(out=o_ps[c][:], lhsT=band_t[:, c, :], rhs=vw[c][:], start=True, stop=True)

        def win_residual(c):
            n = index[("win", c)]
            acc[n] = acc_pool.tile([P, D], F32, name="acc")
            nc.vector.scalar_tensor_tensor(
                out=acc[n][:],
                in0=o_ps[c][:],
                scalar=1.0,
                in1=x_win[c],
                op0=ALU.mult,
                op1=ALU.add,
                accum_out=sum_place(n),
            )

        def squares(n):
            g, a = divmod(n, GRP)
            junk = junk_pool.tile([P, D], BF16, name="junk")
            nc.scalar.activation(
                out=junk[:],
                in_=acc[n][:],
                func=ACT.Square,
                bias=sums[g][:, a : a + 1],
                scale=-1.0 * D,
                accum_out=ssq[g][:, a : a + 1],
            )

        def stats(key, s, q, width):
            mu[key] = stat_pool.tile([P, GRP], F32, name="mu")
            nc.gpsimd.tensor_scalar(
                out=mu[key][:, 0:width], in0=s, scalar1=-1.0 / D, scalar2=0.0, op0=ALU.mult, op1=ALU.add
            )
            var = stat_pool.tile([P, GRP], F32, name="var")
            nc.gpsimd.tensor_scalar(
                out=var[:, 0:width], in0=q, scalar1=1.0 / (D * D * D), scalar2=EPS, op0=ALU.mult, op1=ALU.add
            )
            rstd[key] = stat_pool.tile([P, GRP], F32, name="rstd")
            nc.gpsimd.tensor_tensor(
                out=rstd[key][:, 0:width], in0=var[:, 0:width], in1=mhalf[:, 0:width], op=ALU.pow
            )

        def normalise(n):
            g, a = divmod(n, GRP)
            if a == 0:
                nrm[g] = big_pool.tile([P, GRP, D], F32, name="nrm")
            nc.gpsimd.tensor_scalar(
                out=nrm[g][:, a, :],
                in0=acc[n][:],
                scalar1=mu[g][:, a : a + 1],
                scalar2=rstd[g][:, a : a + 1],
                op0=ALU.add,
                op1=ALU.mult,
            )

        def to_features(g, c):
            f_ps[c] = psf.tile([P, GRP * P], F32, name="f_ps", tag="fb")
            for a in range(GRP):
                nc.tensor.transpose(
                    out=f_ps[c][:, a * P : (a + 1) * P], in_=nrm[g][:, a, c * P : (c + 1) * P], identity=ident_f
                )

        def affine(g, c):
            if c == 0:
                y_t[g] = big_pool.tile([P, GRP, GRP * P], F32, name="y_t")
            nc.scalar.activation(
                out=y_t[g][:, c, :],
                in_=f_ps[c][:],
                func=ACT.Identity,
                scale=gb[:, c : c + 1],
                bias=gb[:, 4 + c : 5 + c],
            )

        def to_rows(g, a):
            b_ps[a] = psf.tile([P, D], F32, name="b_ps", tag="fb")
            for c in range(GRP):
                nc.tensor.transpose(
                    out=b_ps[a][:, c * P : (c + 1) * P], in_=y_t[g][:, c, a * P : (a + 1) * P], identity=ident_f
                )

        def store(n, tile):
            kind, i = order[n]
            if kind == "tap":
                nc.sync.dma_start(out=o_rows[:, i, :], in_=tile)
            else:
                r0 = TAP_ROWS + WIN_OUT * i
                rows = min(WIN_OUT, ROWS - r0)
                p0 = r0 - win_row0(i)
                nc.sync.dma_start(out=of[r0 : r0 + rows, :], in_=tile[p0 : p0 + rows, :])

        def leave(g, a):
            if a == 0:
                o_sb[g] = out_pool.tile([P, GRP, D], F32, name="o_sb")
            nc.scalar.copy(out=o_sb[g][:, a, :], in_=b_ps[a][:])
            store(GRP * g + a, o_sb[g][:, a, :])

        def affine_on_vector(n):
            cen = junk_pool.tile([P, D], F32, name="cen")
            nc.vector.scalar_tensor_tensor(
                out=cen[:], in0=acc[n][:], scalar=mu[("one", n)][:, 0:1], in1=gamma_b[:], op0=ALU.add, op1=ALU.mult
            )
            o_one = out_pool.tile([P, D], F32, name="o_one")
            nc.vector.scalar_tensor_tensor(
                out=o_one[:], in0=cen[:], scalar=rstd[("one", n)][:, 0:1], in1=beta_b[:], op0=ALU.mult, op1=ALU.add
            )
            store(n, o_one[:])

        for k in range(min(KBEG, -4), max(KEND, NS + LAG + 4)):
            if 0 <= k + 2 < NS:
                project(k + 2)
            if 0 <= k - 1 < NS and slots[k - 1][0] == "win":
                win_mix(slots[k - 1][1])
            for g, r in feat_at.get(k, []):
                if r == 0:
                    to_features(g, 0)
                    to_features(g, 1)
                if r == 1:
                    affine(g, 0)
                    affine(g, 1)
                    to_features(g, 2)
                    to_features(g, 3)
                if r == 2:
                    affine(g, 2)
                    affine(g, 3)
                    to_rows(g, 0)
                    to_rows(g, 1)
                if r == 3:
                    leave(g, 0)
                    leave(g, 1)
                    to_rows(g, 2)
                    to_rows(g, 3)
                if r == 4:
                    leave(g, 2)
                    leave(g, 3)
            if k - 1 in job_at:
                job_copy(job_at[k - 1])
            if k in job_at:
                job_turn(job_at[k])
            for n in range(NI):
                if done[n] == k - 1:
                    squares(n)
            if 0 <= k + 4 < NS and slots[k + 4][0] == "tap" and slots[k + 4][1] < RUN:
                bias_part(slots[k + 4][1])
            if 0 <= k + 3 < NS and slots[k + 3][0] == "tap" and slots[k + 3][1] < RUN:
                residual(slots[k + 3][1])
            if k + 1 in job_at and job_at[k + 1][1] == "band":
                band_rows(job_at[k + 1][2])
            for g, r in stat_at.get(k, []):
                if r == 0:
                    stats(g, sums[g][:], ssq[g][:], GRP)
                normalise(GRP * g + r)
            for n in range(GRP * NG_T, NI):
                if done[n] == k - 2:
                    g, a = divmod(n, GRP)
                    stats(("one", n), sums[g][:, a : a + 1], ssq[g][:, a : a + 1], 1)
            if LAG <= k < NS + LAG and slots[k - LAG][0] == "win":
                win_residual(slots[k - LAG][1])
            if 0 <= k < NS:
                if slots[k][0] == "tap":
                    taps(k)
                else:
                    win_leave(k)
            if k == 0:
                band_weights()
            for n in range(GRP * NG_T, NI):
                if done[n] == k - 3:
                    affine_on_vector(n)
            for key in quant_at.get(k, []):
                quantise(key, GRP if key[0] == "tap" else min(2, NW - 2 * key[1]))
